import numpy as np
import ml_dtypes

BF16 = ml_dtypes.bfloat16


def bf(x):
    return np.asarray(x, np.float32).astype(BF16)


def f32(x):
    return np.asarray(x, np.float32)


def f64(x):
    return np.asarray(x).astype(np.float64)


def striped(idx):
    return np.tile(idx.reshape(-1, 16).T, (8, 1))


D, S, M, M2, N = 128, 256, 128, 128, 128


def elu(v):
    return np.where(v > 0.0, v, np.exp(np.minimum(v, 0.0)) - 1.0)


def setup_inputs():
    return {"table": bf(np.abs(np.random.standard_normal((D, S)))), "w0": bf(np.random.standard_normal((D, M)) / np.sqrt(D)), "b0": f32(0.1 * np.random.standard_normal((M, 1))), "w1": bf(np.random.standard_normal((M, M2)) / np.sqrt(M)), "b1": f32(0.1 * np.random.standard_normal((M2, 1))), "offs": striped(np.random.permutation(np.tile(np.arange(S), 2))[:N])}


def reference(table, w0, b0, w1, b1, offs):
    idx = offs[:16].T.reshape(-1)
    h = elu(f64(w0).T @ f64(table)[:, idx] + f64(b0))
    return elu(f64(w1).T @ h + f64(b1))

@@ -1,0 +1,54 @@
+import concourse.mybir as mybir
+
+BF16, F32, U16 = mybir.dt.bfloat16, mybir.dt.float32, mybir.dt.uint16
+ADD, MIN, MAX = mybir.AluOpType.add, mybir.AluOpType.min, mybir.AluOpType.max
+EXP = mybir.ActivationFunctionType.Exp
+
+P = 128
+NODES = 256
+QUERIES = 128
+
+FLOPS = 2 * 2 * P * P * QUERIES
+
+
+def elu_of_product(nc, pool, result, product, bias, layer):
+    negative = pool.tile([P, QUERIES], F32, name=f"negative{layer}")
+    positive = pool.tile([P, QUERIES], F32, name=f"positive{layer}")
+    decayed = pool.tile([P, QUERIES], F32, name=f"decayed{layer}")
+    nc.vector.tensor_scalar(negative[:], product[:], bias[:], 0.0, ADD, MIN)
+    nc.scalar.activation(decayed[:], negative[:], EXP)
+    nc.vector.tensor_scalar(positive[:], product[:], bias[:], 0.0, ADD, MAX)
+    nc.vector.scalar_tensor_tensor(result[:], decayed[:], -1.0, positive[:], ADD, ADD)
+
+
+def tile_densegatperfplayermodel_kernel(tc, table, w0, b0, w1, b1, offs, out):
+    nc = tc.nc
+    with (
+        tc.tile_pool(name="held", bufs=1) as held,
+        tc.psum_pool(name="psum", bufs=1) as psum,
+    ):
+        offsets = held.tile([P, QUERIES // 16], U16, name="offsets")
+        nodes = held.tile([P, NODES], BF16, name="nodes")
+        weights0 = held.tile([P, P], BF16, name="weights0")
+        weights1 = held.tile([P, P], BF16, name="weights1")
+        bias0 = held.tile([P, 1], F32, name="bias0")
+        bias1 = held.tile([P, 1], F32, name="bias1")
+
+        nc.sync.dma_start(offsets[:], offs)
+        nc.scalar.dma_start(weights0[:], w0)
+        nc.sync.dma_start(nodes[:], table)
+        nc.scalar.dma_start(bias0[:], b0)
+        nc.gpsimd.dma_start(weights1[:], w1)
+        nc.gpsimd.dma_start(bias1[:], b1)
+
+        product0 = psum.tile([P, QUERIES], F32, name="product0")
+        nc.tensor.matmul(product0[:], weights0[:], nodes[:].indirect(offsets[:]), start=True, stop=True)
+        hidden = held.tile([P, QUERIES], BF16, name="hidden")
+        elu_of_product(nc, held, hidden, product0, bias0, 0)
+
+        product1 = psum.tile([P, QUERIES], F32, name="product1")
+        nc.tensor.matmul(product1[:], weights1[:], hidden[:], start=True, stop=True)
+        result = held.tile([P, QUERIES], F32, name="result")
+        elu_of_product(nc, held, result, product1, bias1, 1)
+
+        nc.sync.dma_start(out, result[:])

@@ -38,8 +38,8 @@ def tile_densegatperfplayermodel_kernel(tc, table, w0, b0, w1, b1, offs, out):
         nc.scalar.dma_start(weights0[:], w0)
         nc.sync.dma_start(nodes[:], table)
         nc.scalar.dma_start(bias0[:], b0)
-        nc.gpsimd.dma_start(weights1[:], w1)
-        nc.gpsimd.dma_start(bias1[:], b1)
+        nc.sync.dma_start(weights1[:], w1)
+        nc.scalar.dma_start(bias1[:], b1)
 
         product0 = psum.tile([P, QUERIES], F32, name="product0")
         nc.tensor.matmul(product0[:], weights0[:], nodes[:].indirect(offsets[:]), start=True, stop=True)

@@ -1,7 +1,7 @@
 import concourse.mybir as mybir
 
 BF16, F32, U16 = mybir.dt.bfloat16, mybir.dt.float32, mybir.dt.uint16
-ADD, MIN, MAX = mybir.AluOpType.add, mybir.AluOpType.min, mybir.AluOpType.max
+ADD = mybir.AluOpType.add
 EXP = mybir.ActivationFunctionType.Exp
 
 P = 128
@@ -11,13 +11,13 @@ QUERIES = 128
 FLOPS = 2 * 2 * P * P * QUERIES
 
 
-def elu_of_product(nc, pool, result, product, bias, layer):
+def elu(nc, pool, result, v, layer):
     negative = pool.tile([P, QUERIES], F32, name=f"negative{layer}")
     positive = pool.tile([P, QUERIES], F32, name=f"positive{layer}")
     decayed = pool.tile([P, QUERIES], F32, name=f"decayed{layer}")
-    nc.vector.tensor_scalar(negative[:], product[:], bias[:], 0.0, ADD, MIN)
+    nc.vector.tensor_scalar_min(negative[:], v[:], 0.0)
     nc.scalar.activation(decayed[:], negative[:], EXP)
-    nc.vector.tensor_scalar(positive[:], product[:], bias[:], 0.0, ADD, MAX)
+    nc.vector.tensor_scalar_max(positive[:], v[:], 0.0)
     nc.vector.scalar_tensor_tensor(result[:], decayed[:], -1.0, positive[:], ADD, ADD)
 
 
@@ -31,24 +31,29 @@ def tile_densegatperfplayermodel_kernel(tc, table, w0, b0, w1, b1, offs, out):
         nodes = held.tile([P, NODES], BF16, name="nodes")
         weights0 = held.tile([P, P], BF16, name="weights0")
         weights1 = held.tile([P, P], BF16, name="weights1")
-        bias0 = held.tile([P, 1], F32, name="bias0")
-        bias1 = held.tile([P, 1], F32, name="bias1")
+        bias0_row = held.tile([1, P], F32, name="bias0_row")
+        bias1_row = held.tile([1, P], F32, name="bias1_row")
+        ones_row = held.tile([1, QUERIES], F32, name="ones_row")
 
         nc.sync.dma_start(offsets[:], offs)
-        nc.scalar.dma_start(weights0[:], w0)
+        nc.scalar.dma_start(bias0_row[:], b0.rearrange("m one -> one m"))
         nc.sync.dma_start(nodes[:], table)
-        nc.scalar.dma_start(bias0[:], b0)
+        nc.scalar.dma_start(weights0[:], w0)
         nc.sync.dma_start(weights1[:], w1)
-        nc.scalar.dma_start(bias1[:], b1)
+        nc.scalar.dma_start(bias1_row[:], b1.rearrange("m one -> one m"))
+        nc.vector.memset(ones_row[:], 1.0)
 
-        product0 = psum.tile([P, QUERIES], F32, name="product0")
-        nc.tensor.matmul(product0[:], weights0[:], nodes[:].indirect(offsets[:]), start=True, stop=True)
+        v0 = psum.tile([P, QUERIES], F32, name="v0")
+        v1 = psum.tile([P, QUERIES], F32, name="v1")
+
+        nc.tensor.matmul(v0[:], bias0_row[:], ones_row[:], start=True, stop=False)
+        nc.tensor.matmul(v0[:], weights0[:], nodes[:].indirect(offsets[:]), start=False, stop=True)
+        nc.tensor.matmul(v1[:], bias1_row[:], ones_row[:], start=True, stop=False)
         hidden = held.tile([P, QUERIES], BF16, name="hidden")
-        elu_of_product(nc, held, hidden, product0, bias0, 0)
+        elu(nc, held, hidden, v0, 0)
 
-        product1 = psum.tile([P, QUERIES], F32, name="product1")
-        nc.tensor.matmul(product1[:], weights1[:], hidden[:], start=True, stop=True)
+        nc.tensor.matmul(v1[:], weights1[:], hidden[:], start=False, stop=True)
         result = held.tile([P, QUERIES], F32, name="result")
-        elu_of_product(nc, held, result, product1, bias1, 1)
+        elu(nc, held, result, v1, 1)
 
         nc.sync.dma_start(out, result[:])

@@ -1,24 +1,36 @@
 import concourse.mybir as mybir
 
 BF16, F32, U16 = mybir.dt.bfloat16, mybir.dt.float32, mybir.dt.uint16
-ADD = mybir.AluOpType.add
+ADD, MIN, MAX = mybir.AluOpType.add, mybir.AluOpType.min, mybir.AluOpType.max
 EXP = mybir.ActivationFunctionType.Exp
 
 P = 128
 NODES = 256
 QUERIES = 128
+PIECES = 2
+WIDTH = QUERIES // PIECES
 
 FLOPS = 2 * 2 * P * P * QUERIES
 
 
-def elu(nc, pool, result, v, layer):
+def columns(piece):
+    return slice(piece * WIDTH, (piece + 1) * WIDTH)
+
+
+def elu_of_products(nc, pool, result, products, bias, layer):
     negative = pool.tile([P, QUERIES], F32, name=f"negative{layer}")
     positive = pool.tile([P, QUERIES], F32, name=f"positive{layer}")
     decayed = pool.tile([P, QUERIES], F32, name=f"decayed{layer}")
-    nc.vector.tensor_scalar_min(negative[:], v[:], 0.0)
-    nc.scalar.activation(decayed[:], negative[:], EXP)
-    nc.vector.tensor_scalar_max(positive[:], v[:], 0.0)
-    nc.vector.scalar_tensor_tensor(result[:], decayed[:], -1.0, positive[:], ADD, ADD)
+    for piece in range(PIECES):
+        nc.vector.tensor_scalar(negative[:, columns(piece)], products[piece][:], bias[:], 0.0, ADD, MIN)
+    for piece in range(PIECES):
+        nc.scalar.activation(decayed[:, columns(piece)], negative[:, columns(piece)], EXP)
+    for piece in range(PIECES):
+        nc.vector.tensor_scalar(positive[:, columns(piece)], products[piece][:], bias[:], 0.0, ADD, MAX)
+    for piece in range(PIECES):
+        nc.vector.scalar_tensor_tensor(
+            result[:, columns(piece)], decayed[:, columns(piece)], -1.0, positive[:, columns(piece)], ADD, ADD
+        )
 
 
 def tile_densegatperfplayermodel_kernel(tc, table, w0, b0, w1, b1, offs, out):
@@ -31,29 +43,29 @@ def tile_densegatperfplayermodel_kernel(tc, table, w0, b0, w1, b1, offs, out):
         nodes = held.tile([P, NODES], BF16, name="nodes")
         weights0 = held.tile([P, P], BF16, name="weights0")
         weights1 = held.tile([P, P], BF16, name="weights1")
-        bias0_row = held.tile([1, P], F32, name="bias0_row")
-        bias1_row = held.tile([1, P], F32, name="bias1_row")
-        ones_row = held.tile([1, QUERIES], F32, name="ones_row")
+        bias0 = held.tile([P, 1], F32, name="bias0")
+        bias1 = held.tile([P, 1], F32, name="bias1")
 
         nc.sync.dma_start(offsets[:], offs)
-        nc.scalar.dma_start(bias0_row[:], b0.rearrange("m one -> one m"))
-        nc.sync.dma_start(nodes[:], table)
         nc.scalar.dma_start(weights0[:], w0)
+        nc.sync.dma_start(nodes[:], table)
+        nc.scalar.dma_start(bias0[:], b0)
         nc.sync.dma_start(weights1[:], w1)
-        nc.scalar.dma_start(bias1_row[:], b1.rearrange("m one -> one m"))
-        nc.vector.memset(ones_row[:], 1.0)
+        nc.scalar.dma_start(bias1[:], b1)
 
-        v0 = psum.tile([P, QUERIES], F32, name="v0")
-        v1 = psum.tile([P, QUERIES], F32, name="v1")
+        products0 = [psum.tile([P, WIDTH], F32, name=f"product0_{piece}") for piece in range(PIECES)]
+        products1 = [psum.tile([P, WIDTH], F32, name=f"product1_{piece}") for piece in range(PIECES)]
 
-        nc.tensor.matmul(v0[:], bias0_row[:], ones_row[:], start=True, stop=False)
-        nc.tensor.matmul(v0[:], weights0[:], nodes[:].indirect(offsets[:]), start=False, stop=True)
-        nc.tensor.matmul(v1[:], bias1_row[:], ones_row[:], start=True, stop=False)
+        for piece in range(PIECES):
+            listed = offsets[:, piece * (WIDTH // 16) : (piece + 1) * (WIDTH // 16)]
+            nc.tensor.matmul(products0[piece][:], weights0[:], nodes[:].indirect(listed), start=True, stop=True)
         hidden = held.tile([P, QUERIES], BF16, name="hidden")
-        elu(nc, held, hidden, v0, 0)
+        elu_of_products(nc, held, hidden, products0, bias0, 0)
 
-        nc.tensor.matmul(v1[:], weights1[:], hidden[:], start=False, stop=True)
+        for piece in range(PIECES):
+            nc.tensor.matmul(products1[piece][:], weights1[:], hidden[:, columns(piece)], start=True, stop=True)
         result = held.tile([P, QUERIES], F32, name="result")
-        elu(nc, held, result, v1, 1)
+        elu_of_products(nc, held, result, products1, bias1, 1)
 
-        nc.sync.dma_start(out, result[:])
+        for piece, queue in enumerate((nc.sync, nc.scalar)):
+            queue.dma_start(out[:, columns(piece)], result[:, columns(piece)])

@@ -46,12 +46,12 @@ def tile_densegatperfplayermodel_kernel(tc, table, w0, b0, w1, b1, offs, out):
         bias0 = held.tile([P, 1], F32, name="bias0")
         bias1 = held.tile([P, 1], F32, name="bias1")
 
+        nc.scalar.dma_start(nodes[:], table)
         nc.sync.dma_start(offsets[:], offs)
-        nc.scalar.dma_start(weights0[:], w0)
-        nc.sync.dma_start(nodes[:], table)
-        nc.scalar.dma_start(bias0[:], b0)
+        nc.sync.dma_start(weights0[:], w0)
+        nc.sync.dma_start(bias0[:], b0)
         nc.sync.dma_start(weights1[:], w1)
-        nc.scalar.dma_start(bias1[:], b1)
+        nc.sync.dma_start(bias1[:], b1)
 
         products0 = [psum.tile([P, WIDTH], F32, name=f"product0_{piece}") for piece in range(PIECES)]
         products1 = [psum.tile([P, WIDTH], F32, name=f"product1_{piece}") for piece in range(PIECES)]

@@ -46,12 +46,12 @@ def tile_densegatperfplayermodel_kernel(tc, table, w0, b0, w1, b1, offs, out):
         bias0 = held.tile([P, 1], F32, name="bias0")
         bias1 = held.tile([P, 1], F32, name="bias1")
 
-        nc.scalar.dma_start(nodes[:], table)
         nc.sync.dma_start(offsets[:], offs)
-        nc.sync.dma_start(weights0[:], w0)
-        nc.sync.dma_start(bias0[:], b0)
+        nc.scalar.dma_start(bias0[:], b0)
+        nc.sync.dma_start(nodes[:], table)
+        nc.scalar.dma_start(weights0[:], w0)
         nc.sync.dma_start(weights1[:], w1)
-        nc.sync.dma_start(bias1[:], b1)
+        nc.scalar.dma_start(bias1[:], b1)
 
         products0 = [psum.tile([P, WIDTH], F32, name=f"product0_{piece}") for piece in range(PIECES)]
         products1 = [psum.tile([P, WIDTH], F32, name=f"product1_{piece}") for piece in range(PIECES)]

@@ -47,9 +47,9 @@ def tile_densegatperfplayermodel_kernel(tc, table, w0, b0, w1, b1, offs, out):
         bias1 = held.tile([P, 1], F32, name="bias1")
 
         nc.sync.dma_start(offsets[:], offs)
+        nc.scalar.dma_start(nodes[:], table)
+        nc.sync.dma_start(weights0[:], w0)
         nc.scalar.dma_start(bias0[:], b0)
-        nc.sync.dma_start(nodes[:], table)
-        nc.scalar.dma_start(weights0[:], w0)
         nc.sync.dma_start(weights1[:], w1)
         nc.scalar.dma_start(bias1[:], b1)
 

@@ -50,8 +50,8 @@ def tile_densegatperfplayermodel_kernel(tc, table, w0, b0, w1, b1, offs, out):
         nc.scalar.dma_start(nodes[:], table)
         nc.sync.dma_start(weights0[:], w0)
         nc.scalar.dma_start(bias0[:], b0)
-        nc.sync.dma_start(weights1[:], w1)
-        nc.scalar.dma_start(bias1[:], b1)
+        nc.sync.dma_start(bias1[:], b1)
+        nc.scalar.dma_start(weights1[:], w1)
 
         products0 = [psum.tile([P, WIDTH], F32, name=f"product0_{piece}") for piece in range(PIECES)]
         products1 = [psum.tile([P, WIDTH], F32, name=f"product1_{piece}") for piece in range(PIECES)]

@@ -2,7 +2,7 @@ import concourse.mybir as mybir
 
 BF16, F32, U16 = mybir.dt.bfloat16, mybir.dt.float32, mybir.dt.uint16
 ADD, MIN, MAX = mybir.AluOpType.add, mybir.AluOpType.min, mybir.AluOpType.max
-EXP = mybir.ActivationFunctionType.Exp
+EXP, RELU = mybir.ActivationFunctionType.Exp, mybir.ActivationFunctionType.Relu
 
 P = 128
 NODES = 256
@@ -18,18 +18,14 @@ def columns(piece):
 
 
 def elu_of_products(nc, pool, result, products, bias, layer):
-    negative = pool.tile([P, QUERIES], F32, name=f"negative{layer}")
+    grown = pool.tile([P, QUERIES], F32, name=f"grown{layer}")
     positive = pool.tile([P, QUERIES], F32, name=f"positive{layer}")
-    decayed = pool.tile([P, QUERIES], F32, name=f"decayed{layer}")
     for piece in range(PIECES):
-        nc.vector.tensor_scalar(negative[:, columns(piece)], products[piece][:], bias[:], 0.0, ADD, MIN)
-    for piece in range(PIECES):
-        nc.scalar.activation(decayed[:, columns(piece)], negative[:, columns(piece)], EXP)
-    for piece in range(PIECES):
-        nc.vector.tensor_scalar(positive[:, columns(piece)], products[piece][:], bias[:], 0.0, ADD, MAX)
+        nc.scalar.activation(grown[:, columns(piece)], products[piece][:], EXP, bias=bias[:])
+        nc.scalar.activation(positive[:, columns(piece)], products[piece][:], RELU, bias=bias[:])
     for piece in range(PIECES):
         nc.vector.scalar_tensor_tensor(
-            result[:, columns(piece)], decayed[:, columns(piece)], -1.0, positive[:, columns(piece)], ADD, ADD
+            result[:, columns(piece)], grown[:, columns(piece)], -1.0, positive[:, columns(piece)], ADD, MIN
         )
 
 
@@ -52,6 +48,10 @@ def tile_densegatperfplayermodel_kernel(tc, table, w0, b0, w1, b1, offs, out):
         nc.scalar.dma_start(bias0[:], b0)
         nc.sync.dma_start(bias1[:], b1)
         nc.scalar.dma_start(weights1[:], w1)
+
+        warm = held.tile([P, 1], F32, name="warm")
+        nc.vector.memset(warm[:], 0.0)
+        nc.scalar.activation(warm[:], warm[:], EXP)
 
         products0 = [psum.tile([P, WIDTH], F32, name=f"product0_{piece}") for piece in range(PIECES)]
         products1 = [psum.tile([P, WIDTH], F32, name=f"product1_{piece}") for piece in range(PIECES)]

@@ -1,14 +1,18 @@
 import concourse.mybir as mybir
 
 BF16, F32, U16 = mybir.dt.bfloat16, mybir.dt.float32, mybir.dt.uint16
-ADD, MIN, MAX = mybir.AluOpType.add, mybir.AluOpType.min, mybir.AluOpType.max
+ADD, MIN = mybir.AluOpType.add, mybir.AluOpType.min
 EXP, RELU = mybir.ActivationFunctionType.Exp, mybir.ActivationFunctionType.Relu
 
 P = 128
 NODES = 256
 QUERIES = 128
-PIECES = 2
-WIDTH = QUERIES // PIECES
+LOOKUPS = 2
+LISTED = QUERIES // LOOKUPS
+STEPS = 2
+WIDTH = QUERIES // STEPS
+STORES = 2
+STORED = QUERIES // STORES
 
 FLOPS = 2 * 2 * P * P * QUERIES
 
@@ -20,10 +24,10 @@ def columns(piece):
 def elu_of_products(nc, pool, result, products, bias, layer):
     grown = pool.tile([P, QUERIES], F32, name=f"grown{layer}")
     positive = pool.tile([P, QUERIES], F32, name=f"positive{layer}")
-    for piece in range(PIECES):
-        nc.scalar.activation(grown[:, columns(piece)], products[piece][:], EXP, bias=bias[:])
-        nc.scalar.activation(positive[:, columns(piece)], products[piece][:], RELU, bias=bias[:])
-    for piece in range(PIECES):
+    for piece in range(STEPS):
+        nc.scalar.activation(grown[:, columns(piece)], products[piece], EXP, bias=bias[:])
+        nc.scalar.activation(positive[:, columns(piece)], products[piece], RELU, bias=bias[:])
+    for piece in range(STEPS):
         nc.vector.scalar_tensor_tensor(
             result[:, columns(piece)], grown[:, columns(piece)], -1.0, positive[:, columns(piece)], ADD, MIN
         )
@@ -42,9 +46,9 @@ def tile_densegatperfplayermodel_kernel(tc, table, w0, b0, w1, b1, offs, out):
         bias0 = held.tile([P, 1], F32, name="bias0")
         bias1 = held.tile([P, 1], F32, name="bias1")
 
-        nc.sync.dma_start(offsets[:], offs)
-        nc.scalar.dma_start(nodes[:], table)
         nc.sync.dma_start(weights0[:], w0)
+        nc.scalar.dma_start(nodes[:], table)
+        nc.sync.dma_start(offsets[:], offs)
         nc.scalar.dma_start(bias0[:], b0)
         nc.sync.dma_start(bias1[:], b1)
         nc.scalar.dma_start(weights1[:], w1)
@@ -53,19 +57,31 @@ def tile_densegatperfplayermodel_kernel(tc, table, w0, b0, w1, b1, offs, out):
         nc.vector.memset(warm[:], 0.0)
         nc.scalar.activation(warm[:], warm[:], EXP)
 
-        products0 = [psum.tile([P, WIDTH], F32, name=f"product0_{piece}") for piece in range(PIECES)]
-        products1 = [psum.tile([P, WIDTH], F32, name=f"product1_{piece}") for piece in range(PIECES)]
+        looked_up = [psum.tile([P, LISTED], F32, name=f"looked_up{half}") for half in range(LOOKUPS)]
+        for half in range(LOOKUPS):
+            listed = offsets[:, half * (LISTED // 16) : (half + 1) * (LISTED // 16)]
+            nc.tensor.matmul(looked_up[half][:], weights0[:], nodes[:].indirect(listed), start=True, stop=True)
+        products0 = [
+            looked_up[piece * WIDTH // LISTED][:, piece * WIDTH % LISTED : piece * WIDTH % LISTED + WIDTH]
+            for piece in range(STEPS)
+        ]
+        grown = held.tile([P, QUERIES], F32, name="grown")
+        hidden_positive = held.tile([P, QUERIES], BF16, name="hidden_positive")
+        hidden_negative = held.tile([P, QUERIES], BF16, name="hidden_negative")
+        for piece in range(STEPS):
+            nc.scalar.activation(grown[:, columns(piece)], products0[piece], EXP, bias=bias0[:])
+            nc.scalar.activation(hidden_positive[:, columns(piece)], products0[piece], RELU, bias=bias0[:])
+        for piece in range(STEPS):
+            nc.vector.tensor_scalar(hidden_negative[:, columns(piece)], grown[:, columns(piece)], -1.0, 0.0, ADD, MIN)
 
-        for piece in range(PIECES):
-            listed = offsets[:, piece * (WIDTH // 16) : (piece + 1) * (WIDTH // 16)]
-            nc.tensor.matmul(products0[piece][:], weights0[:], nodes[:].indirect(listed), start=True, stop=True)
-        hidden = held.tile([P, QUERIES], BF16, name="hidden")
-        elu_of_products(nc, held, hidden, products0, bias0, 0)
-
-        for piece in range(PIECES):
-            nc.tensor.matmul(products1[piece][:], weights1[:], hidden[:, columns(piece)], start=True, stop=True)
+        banks1 = [psum.tile([P, WIDTH], F32, name=f"bank1_{piece}") for piece in range(STEPS)]
+        for piece in range(STEPS):
+            nc.tensor.matmul(banks1[piece][:], weights1[:], hidden_positive[:, columns(piece)], start=True, stop=False)
+            nc.tensor.matmul(banks1[piece][:], weights1[:], hidden_negative[:, columns(piece)], start=False, stop=True)
         result = held.tile([P, QUERIES], F32, name="result")
-        elu_of_products(nc, held, result, products1, bias1, 1)
+        elu_of_products(nc, held, result, [bank[:] for bank in banks1], bias1, 1)
 
-        for piece, queue in enumerate((nc.sync, nc.scalar)):
-            queue.dma_start(out[:, columns(piece)], result[:, columns(piece)])
+        for store in range(STORES):
+            queue = (nc.sync, nc.scalar)[store % 2]
+            stored = slice(store * STORED, (store + 1) * STORED)
+            queue.dma_start(out[:, stored], result[:, stored])

@@ -46,8 +46,8 @@ def tile_densegatperfplayermodel_kernel(tc, table, w0, b0, w1, b1, offs, out):
         bias0 = held.tile([P, 1], F32, name="bias0")
         bias1 = held.tile([P, 1], F32, name="bias1")
 
-        nc.sync.dma_start(weights0[:], w0)
-        nc.scalar.dma_start(nodes[:], table)
+        nc.sync.dma_start(nodes[:], table)
+        nc.scalar.dma_start(weights0[:], w0)
         nc.sync.dma_start(offsets[:], offs)
         nc.scalar.dma_start(bias0[:], b0)
         nc.sync.dma_start(bias1[:], b1)

import concourse.mybir as mybir

BF16, F32, U16 = mybir.dt.bfloat16, mybir.dt.float32, mybir.dt.uint16
ADD, MIN = mybir.AluOpType.add, mybir.AluOpType.min
EXP, RELU = mybir.ActivationFunctionType.Exp, mybir.ActivationFunctionType.Relu

P = 128
NODES = 256
QUERIES = 128
LOOKUPS = 2
LISTED = QUERIES // LOOKUPS
STEPS = 2
WIDTH = QUERIES // STEPS
STORES = 2
STORED = QUERIES // STORES

FLOPS = 2 * 2 * P * P * QUERIES


def columns(piece):
    return slice(piece * WIDTH, (piece + 1) * WIDTH)


def elu_of_products(nc, pool, result, products, bias, layer):
    grown = pool.tile([P, QUERIES], F32, name=f"grown{layer}")
    positive = pool.tile([P, QUERIES], F32, name=f"positive{layer}")
    for piece in range(STEPS):
        nc.scalar.activation(grown[:, columns(piece)], products[piece], EXP, bias=bias[:])
        nc.scalar.activation(positive[:, columns(piece)], products[piece], RELU, bias=bias[:])
    for piece in range(STEPS):
        nc.vector.scalar_tensor_tensor(
            result[:, columns(piece)], grown[:, columns(piece)], -1.0, positive[:, columns(piece)], ADD, MIN
        )


def tile_densegatperfplayermodel_kernel(tc, table, w0, b0, w1, b1, offs, out):
    nc = tc.nc
    with (
        tc.tile_pool(name="held", bufs=1) as held,
        tc.psum_pool(name="psum", bufs=1) as psum,
    ):
        offsets = held.tile([P, QUERIES // 16], U16, name="offsets")
        nodes = held.tile([P, NODES], BF16, name="nodes")
        weights0 = held.tile([P, P], BF16, name="weights0")
        weights1 = held.tile([P, P], BF16, name="weights1")
        bias0 = held.tile([P, 1], F32, name="bias0")
        bias1 = held.tile([P, 1], F32, name="bias1")

        nc.sync.dma_start(nodes[:], table)
        nc.scalar.dma_start(weights0[:], w0)
        nc.sync.dma_start(offsets[:], offs)
        nc.scalar.dma_start(bias0[:], b0)
        nc.sync.dma_start(bias1[:], b1)
        nc.scalar.dma_start(weights1[:], w1)

        warm = held.tile([P, 1], F32, name="warm")
        nc.vector.memset(warm[:], 0.0)
        nc.scalar.activation(warm[:], warm[:], EXP)

        looked_up = [psum.tile([P, LISTED], F32, name=f"looked_up{half}") for half in range(LOOKUPS)]
        for half in range(LOOKUPS):
            listed = offsets[:, half * (LISTED // 16) : (half + 1) * (LISTED // 16)]
            nc.tensor.matmul(looked_up[half][:], weights0[:], nodes[:].indirect(listed), start=True, stop=True)
        products0 = [
            looked_up[piece * WIDTH // LISTED][:, piece * WIDTH % LISTED : piece * WIDTH % LISTED + WIDTH]
            for piece in range(STEPS)
        ]
        grown = held.tile([P, QUERIES], F32, name="grown")
        hidden_positive = held.tile([P, QUERIES], BF16, name="hidden_positive")
        hidden_negative = held.tile([P, QUERIES], BF16, name="hidden_negative")
        for piece in range(STEPS):
            nc.scalar.activation(grown[:, columns(piece)], products0[piece], EXP, bias=bias0[:])
            nc.scalar.activation(hidden_positive[:, columns(piece)], products0[piece], RELU, bias=bias0[:])
        for piece in range(STEPS):
            nc.vector.tensor_scalar(hidden_negative[:, columns(piece)], grown[:, columns(piece)], -1.0, 0.0, ADD, MIN)

        banks1 = [psum.tile([P, WIDTH], F32, name=f"bank1_{piece}") for piece in range(STEPS)]
        for piece in range(STEPS):
            nc.tensor.matmul(banks1[piece][:], weights1[:], hidden_positive[:, columns(piece)], start=True, stop=False)
            nc.tensor.matmul(banks1[piece][:], weights1[:], hidden_negative[:, columns(piece)], start=False, stop=True)
        result = held.tile([P, QUERIES], F32, name="result")
        elu_of_products(nc, held, result, [bank[:] for bank in banks1], bias1, 1)

        for store in range(STORES):
            queue = (nc.sync, nc.scalar)[store % 2]
            stored = slice(store * STORED, (store + 1) * STORED)
            queue.dma_start(out[:, stored], result[:, stored])
